import numpy as np
import ml_dtypes


def mxq(x, axis, fmt="e4m3"):
    dtype, down = {"e4m3": (ml_dtypes.float8_e4m3fn, 7), "e5m2": (ml_dtypes.float8_e5m2, 14)}[fmt]
    v = np.moveaxis(np.asarray(x, np.float32).astype(ml_dtypes.bfloat16).astype(np.float64), axis, -1)
    blocks = v.reshape(v.shape[:-1] + (-1, 32))
    amax = np.abs(blocks).max(-1, keepdims=True)
    byte = np.maximum(np.where(amax > 0, np.frexp(amax)[1] - 1 + 127, 0) - down, 1)
    scale = np.exp2(byte - 127.0)
    codes = (blocks / scale).astype(np.float32).astype(dtype).astype(np.float64)
    return np.moveaxis((codes * scale).reshape(v.shape), -1, axis)


WIDE = False


def mx_kscale(k):
    if not WIDE:
        return np.ones(k)
    levels = np.array([30, -30])
    if k % 512:
        return np.exp2(np.random.permutation(np.resize(levels, k // 32))).repeat(32)
    a = np.empty((k // 512, 16))
    for p in range(k // 512):
        a[p, :8] = np.random.permutation(np.resize(levels, 8))
        for g in range(8):
            far = levels[np.abs(levels - a[p, g]) >= 10]
            a[p, g + 8] = far[np.random.randint(len(far))]
    return np.exp2(a.ravel()).repeat(32)


BF16 = ml_dtypes.bfloat16


def bf(x):
    return np.asarray(x, np.float32).astype(BF16)


def f64(x):
    return np.asarray(x).astype(np.float64)


E2M1 = np.array([0.0, 0.5, 1.0, 1.5, 2.0, 3.0, 4.0, 6.0, -0.0, -0.5, -1.0, -1.5, -2.0, -3.0, -4.0, -6.0])


def pack_weight(w, fmt):
    k, n = w.shape
    w = f64(bf(w)).reshape(k // 32, 32, n)
    amax = np.abs(w).max(1)
    if fmt == "e4m3":
        byte = np.frexp(amax)[1] - 1 + 127 - 7
    else:
        mant, ex = np.frexp(amax / 6.0)
        byte = np.where(mant > 0.5, ex, ex - 1) + 127
    byte = np.clip(np.where(amax > 0, byte, 1), 1, 254)
    scaled = (w * np.exp2(127.0 - byte)[:, None, :]).reshape(k, n).astype(np.float32)
    by_word = np.ascontiguousarray(scaled.reshape(k // 512, 128, 4, n).transpose(0, 1, 3, 2))
    if fmt == "e4m3":
        words = by_word.astype(ml_dtypes.float8_e4m3fn).view(np.uint8)
    else:
        c = by_word.astype(ml_dtypes.float4_e2m1fn).view(np.uint8) & 0xF
        words = c[..., 0::2] | (c[..., 1::2] << 4)
    return np.ascontiguousarray(words), np.ascontiguousarray(byte.astype(np.uint8).reshape(k // 512, 16, n))


def unpack_weight(words, scales, fmt):
    g, p, n, _ = words.shape
    if fmt == "e4m3":
        vals = np.ascontiguousarray(words).view(ml_dtypes.float8_e4m3fn).astype(np.float64)
    else:
        nib = np.empty((g, p, n, 4), np.uint8)
        nib[..., 0::2] = words & 0xF
        nib[..., 1::2] = words >> 4
        vals = E2M1[nib]
    vals = vals * np.repeat(np.exp2(scales.astype(np.float64) - 127.0), 8, axis=1)[..., None]
    return vals.transpose(0, 1, 3, 2).reshape(g * 512, n)

def pack4(w):
    words, scales = pack_weight(w, "e2m1")
    return words.reshape(words.shape[0], 128, -1), scales


def unpack4(words, scales):
    return unpack_weight(words.reshape(words.shape[0], 128, -1, 2), scales, "e2m1")


B, S, HID, H, KV, D, ROT, D_PAD = 8, 2048, 512, 2, 2, 32, 16, 128
T = B * S
HALF = ROT // 2
NQ = H * D
NK = KV * D


def partial_rope(x, cos, sin):
    x1 = x[:, :, :HALF]
    x2 = x[:, :, HALF:ROT]
    xp = x[:, :, ROT:]
    c = cos[:, None, :]
    s = sin[:, None, :]
    return np.concatenate([x1 * c - x2 * s, x2 * c + x1 * s, xp], axis=-1)


def setup_inputs():
    s = mx_kscale(HID)
    hidden_states = bf(np.random.standard_normal((T, HID)) * s)
    cos = bf(np.random.uniform(size=(T, HALF)))
    sin = bf(np.random.uniform(size=(T, HALF)))
    w_qk = np.random.standard_normal((NQ + NK, HID)) / np.sqrt(HID) / s[None, :]
    words, scales = pack4(np.ascontiguousarray(w_qk.T))
    b_qk = bf(np.random.standard_normal(NQ + NK) * 0.3)
    return {"hidden_states": hidden_states,
            "cos": cos,
            "sin": sin,
            "w_qk_words": words,
            "w_qk_scales": scales,
            "b_qk": b_qk}


def reference(hidden_states, cos, sin, w_qk_words, w_qk_scales, b_qk):
    qk = (mxq(f64(hidden_states), 1, "e5m2") @ unpack4(w_qk_words, w_qk_scales)) + f64(b_qk)
    q = qk[:, :NQ].reshape(T, H, D)
    k = qk[:, NQ:].reshape(T, KV, D)
    c = f64(cos)
    s = f64(sin)
    return partial_rope(q, c, s), partial_rope(k, c, s)

@@ -1,0 +1,192 @@
+from contextlib import ExitStack
+
+import concourse.mybir as mybir
+from concourse.masks import make_identity
+
+T, HID, NOUT = 16384, 512, 128
+HEAD, HALF = 32, 8
+FLOPS = 2 * T * HID * NOUT
+
+F32 = mybir.dt.float32
+BF16 = mybir.dt.bfloat16
+I32 = mybir.dt.int32
+U32 = mybir.dt.uint32
+U8 = mybir.dt.uint8
+E5M2X4 = mybir.dt.float8_e5m2_x4
+E2M1X4 = mybir.dt.float4_e2m1fn_x4
+ALU = mybir.AluOpType
+
+P = 128
+TILES = T // P
+PAIR = 2
+QUAD = 4
+STORES = [[2, 2, 4, 8]] + [[8, 8]] * 6 + [[8], [4], [2], [2]]
+X_BUFS = 12
+
+
+def tile_flashphiattention_pa_t_kernel(tc, hidden_states, cos, sin, w_qk_words, w_qk_scales, b_qk, out_0, out_1):
+    nc = tc.nc
+    groups = []
+    first = 0
+    for s, sizes in enumerate(STORES):
+        within = 0
+        for n in sizes:
+            groups.append((first, n, s, within))
+            first += n
+            within += n
+    assert first == TILES
+    n_groups = len(groups)
+
+    x_hbm = hidden_states.rearrange("(p j) k -> p j k", p=P)
+    out_hbm = [o.rearrange("(p j) h d -> p j (h d)", p=P) for o in (out_0, out_1)]
+
+    with ExitStack() as ctx:
+        const = ctx.enter_context(tc.tile_pool(name="const", bufs=1))
+        x_pool = ctx.enter_context(tc.tile_pool(name="x", bufs=X_BUFS))
+        mx_pool = ctx.enter_context(tc.tile_pool(name="mx", bufs=3))
+        out_pool = ctx.enter_context(tc.tile_pool(name="out", bufs=6))
+        xt_psum = ctx.enter_context(tc.psum_pool(name="xt", bufs=4))
+        qk_psum = ctx.enter_context(tc.psum_pool(name="qk", bufs=4))
+        ctx.enter_context(tc.manual_schedule())
+
+        ident = const.tile([P, P], F32, name="ident")
+        w_words = const.tile([P, 2 * NOUT], U8, name="w_words", align_bytes=64)
+        w_scales = const.tile([P, 4, NOUT], U8, name="w_scales", align_bytes=64)
+        bias_row = const.tile([P, NOUT], BF16, name="bias_row")
+        ones = const.tile([P, P], BF16, name="ones")
+        bias = const.tile([P, NOUT], F32, name="bias")
+        cos_sb = const.tile([P, TILES, HALF], BF16, name="cos_sb")
+        sin_sb = const.tile([P, TILES, HALF], BF16, name="sin_sb")
+
+        x_sb, grouped, codes, scales, qk, out_sb, prod = {}, {}, {}, {}, {}, {}, {}
+
+        def load(g):
+            j0, n = groups[g][:2]
+            x_sb[g] = x_pool.tile([P, n, HID], BF16, name="x_sb")
+            nc.sync.dma_start(out=x_sb[g][:], in_=x_hbm[:, j0 : j0 + n, :])
+
+        def transpose(g):
+            n = groups[g][1]
+            grouped[g] = mx_pool.tile([P, n * HID], BF16, name="grouped", align_bytes=64)
+            words = x_sb[g][:].rearrange("p i k -> p (i k)").bitcast(F32)
+            dst = grouped[g][:].bitcast(F32).rearrange("p (i r u) -> p i r u", r=P, u=2)
+            for i0 in range(0, n, PAIR):
+                xt = xt_psum.tile([P, PAIR, 2, P], F32, name="xt")
+                for i in range(PAIR):
+                    w0 = (i0 + i) * (HID // 2)
+                    for u in range(2):
+                        nc.tensor.transpose(xt[:, i, u, :], words[:, w0 + u : w0 + HID // 2 : 2], ident[:])
+                nc.scalar.copy(out=dst[:, i0 : i0 + PAIR, :, :], in_=xt[:].rearrange("p i u r -> p i r u"))
+
+        def quantize(g):
+            n = groups[g][1]
+            codes[g] = mx_pool.tile([P, n * P], U32, name="codes", align_bytes=64)
+            scales[g] = mx_pool.tile([P, n * P], U8, name="scales", align_bytes=64)
+            nc.vector.quantize_mx(out=codes[g][:].bitcast(E5M2X4), scales=scales[g][:], in_=grouped[g][:])
+
+        def project(g):
+            n = groups[g][1]
+            qk[g] = []
+            for i0 in range(0, n, QUAD):
+                m = min(QUAD, n - i0)
+                bank = qk_psum.tile([P, m, NOUT], F32, name="bank")
+                for i in range(m):
+                    cols = slice((i0 + i) * P, (i0 + i + 1) * P)
+                    nc.tensor.matmul_mx(
+                        out=bank[:, i, :],
+                        lhsT=codes[g][:, cols].bitcast(E5M2X4),
+                        lhsT_scale=scales[g][:, cols],
+                        rhs=w_words[:].bitcast(E2M1X4),
+                        rhs_scale=w_scales[:, 0, :],
+                        start=True,
+                        stop=True,
+                    )
+                qk[g].append((i0, m, bank))
+
+        def add_bias(g):
+            s, within = groups[g][2:]
+            if within == 0:
+                out_sb[s] = out_pool.tile([P, 2, sum(STORES[s]), NOUT // 2], F32, name="out_sb")
+            for i0, m, bank in qk[g]:
+                nc.vector.tensor_tensor(
+                    out=out_sb[s][:, :, within + i0 : within + i0 + m, :],
+                    in0=bank[:].rearrange("p i (a c) -> p a i c", a=2),
+                    in1=bias[:].rearrange("p (a c) -> p a c", a=2).unsqueeze(2).broadcast_to([P, 2, m, NOUT // 2]),
+                    op=ALU.add,
+                )
+
+        def heads(g):
+            n, s, within = groups[g][1:]
+            return out_sb[s][:, :, within : within + n, :].rearrange("p a i (h d) -> p a i h d", d=HEAD)
+
+        def multiply(g):
+            j0, n = groups[g][:2]
+            prod[g] = mx_pool.tile([P, 2, 2, n, 2, 2, HALF], F32, name="prod")
+            for t, table in enumerate((cos_sb, sin_sb)):
+                factor = table[:, j0 : j0 + n, :].unsqueeze(2).broadcast_to([P, n, 4, HALF])
+                for a in range(2):
+                    nc.vector.tensor_tensor(
+                        out=prod[g][:, t, a, :, :, :, :].rearrange("p i h f j -> p i (h f) j"),
+                        in0=heads(g)[:, a, :, :, 0 : 2 * HALF],
+                        in1=factor,
+                        op=ALU.mult,
+                    )
+
+        def combine(g):
+            n, s, within = groups[g][1:]
+            nc.vector.tensor_tensor(
+                out=heads(g)[:, :, :, :, 0:HALF],
+                in0=prod[g][:, 0, :, :, :, 0, :],
+                in1=prod[g][:, 1, :, :, :, 1, :],
+                op=ALU.subtract,
+            )
+            nc.vector.tensor_tensor(
+                out=heads(g)[:, :, :, :, HALF : 2 * HALF],
+                in0=prod[g][:, 0, :, :, :, 1, :],
+                in1=prod[g][:, 1, :, :, :, 0, :],
+                op=ALU.add,
+            )
+            if within + n == sum(STORES[s]):
+                j1 = groups[g][0] + n
+                for a in range(2):
+                    nc.sync.dma_start(out=out_hbm[a][:, j1 - within - n : j1, :], in_=out_sb[s][:, a, :, :])
+
+        make_identity(nc, ident[:])
+        nc.vector.memset(bias_row[:], 0.0)
+        nc.vector.memset(ones[:], 1.0)
+        load(0)
+        nc.sync.dma_start(out=w_words[:].bitcast(I32), in_=w_qk_words[0].bitcast(I32))
+        nc.sync.dma_start(
+            out=w_scales[0:4, :, :].bitcast(I32),
+            in_=w_qk_scales[0].rearrange("(q r) n -> r q n", r=4).bitcast(I32),
+        )
+        nc.sync.dma_start(out=bias_row[0:1, :], in_=b_qk.rearrange("(o n) -> o n", o=1))
+        load(1)
+        load(2)
+        nc.sync.dma_start(out=cos_sb[:], in_=cos.rearrange("(p j) c -> p j c", p=P))
+        nc.sync.dma_start(out=sin_sb[:], in_=sin.rearrange("(p j) c -> p j c", p=P))
+        for g in range(3, X_BUFS):
+            load(g)
+        for q in range(1, 4):
+            nc.vector.tensor_copy(
+                out=w_scales[32 * q : 32 * q + 4, 0, :].bitcast(I32), in_=w_scales[0:4, q, :].bitcast(I32)
+            )
+
+        for i in range(-3, n_groups + 1):
+            if 0 <= i < n_groups:
+                add_bias(i)
+            if 0 <= i - 1 < n_groups:
+                combine(i - 1)
+            if i + 3 < n_groups:
+                transpose(i + 3)
+                if i + 3 + X_BUFS < n_groups:
+                    load(i + 3 + X_BUFS)
+            if i == -2:
+                spread = qk_psum.tile([P, NOUT], F32, name="bank")
+                nc.tensor.matmul(spread[:], lhsT=ones[:], rhs=bias_row[:], start=True, stop=True)
+                nc.vector.tensor_copy(out=bias[:], in_=spread[:])
+            if 0 <= i + 2 < n_groups:
+                quantize(i + 2)
+                project(i + 2)
+            if 0 <= i < n_groups:
+                multiply(i)

@@ -20,20 +20,22 @@ P = 128
 TILES = T // P
 PAIR = 2
 QUAD = 4
-STORES = [[2, 2, 4, 8]] + [[8, 8]] * 6 + [[8], [4], [2], [2]]
-X_BUFS = 12
+GROUPS = [2, 2, 4] + [8] * 14 + [4, 4]
+LOADS = [2, 2] + [4] * 31
+EARLY = 16
+SHARED = range(3, 17)
+T_LEAD = 8
+Q_LEAD = 4
+X_BUFS = 16
 
 
 def tile_flashphiattention_pa_t_kernel(tc, hidden_states, cos, sin, w_qk_words, w_qk_scales, b_qk, out_0, out_1):
     nc = tc.nc
     groups = []
     first = 0
-    for s, sizes in enumerate(STORES):
-        within = 0
-        for n in sizes:
-            groups.append((first, n, s, within))
-            first += n
-            within += n
+    for n in GROUPS:
+        groups.append((first, n))
+        first += n
     assert first == TILES
     n_groups = len(groups)
 
@@ -44,7 +46,9 @@ def tile_flashphiattention_pa_t_kernel(tc, hidden_states, cos, sin, w_qk_words, 
         const = ctx.enter_context(tc.tile_pool(name="const", bufs=1))
         x_pool = ctx.enter_context(tc.tile_pool(name="x", bufs=X_BUFS))
         mx_pool = ctx.enter_context(tc.tile_pool(name="mx", bufs=3))
-        out_pool = ctx.enter_context(tc.tile_pool(name="out", bufs=6))
+        out_pool = ctx.enter_context(tc.tile_pool(name="out", bufs=14))
+        grp_pool = ctx.enter_context(tc.tile_pool(name="grp", bufs=4))
+        fac_pool = ctx.enter_context(tc.tile_pool(name="fac", bufs=6))
         xt_psum = ctx.enter_context(tc.psum_pool(name="xt", bufs=4))
         qk_psum = ctx.enter_context(tc.psum_pool(name="qk", bufs=4))
         ctx.enter_context(tc.manual_schedule())
@@ -55,28 +59,36 @@ def tile_flashphiattention_pa_t_kernel(tc, hidden_states, cos, sin, w_qk_words, 
         bias_row = const.tile([P, NOUT], BF16, name="bias_row")
         ones = const.tile([P, P], BF16, name="ones")
         bias = const.tile([P, NOUT], F32, name="bias")
-        cos_sb = const.tile([P, TILES, HALF], BF16, name="cos_sb")
-        sin_sb = const.tile([P, TILES, HALF], BF16, name="sin_sb")
+        cos_sin_early = const.tile([P, 2, EARLY, HALF], BF16, name="cos_sin_early")
+        cos_sin_late = const.tile([P, 2, TILES - EARLY, HALF], BF16, name="cos_sin_late")
 
-        x_sb, grouped, codes, scales, qk, out_sb, prod = {}, {}, {}, {}, {}, {}, {}
+        x_sb, grouped, codes, scales, qk, out_sb, prod, factors = {}, {}, {}, {}, {}, {}, {}, {}
 
-        def load(g):
-            j0, n = groups[g][:2]
-            x_sb[g] = x_pool.tile([P, n, HID], BF16, name="x_sb")
-            nc.sync.dma_start(out=x_sb[g][:], in_=x_hbm[:, j0 : j0 + n, :])
+        load_first = [sum(LOADS[:c]) for c in range(len(LOADS))]
+        group_of = [g for g, n in enumerate(GROUPS) for i in range(n)]
+        load_of = [c for c, n in enumerate(LOADS) for i in range(n)]
 
-        def transpose(g):
-            n = groups[g][1]
-            grouped[g] = mx_pool.tile([P, n * HID], BF16, name="grouped", align_bytes=64)
-            words = x_sb[g][:].rearrange("p i k -> p (i k)").bitcast(F32)
+        def load(c):
+            x_sb[c] = x_pool.tile([P, LOADS[c], HID], BF16, name="x_sb")
+            nc.sync.dma_start(out=x_sb[c][:], in_=x_hbm[:, load_first[c] : load_first[c] + LOADS[c], :])
+
+        def transpose(j0):
+            g, c = group_of[j0], load_of[j0]
+            first, n = groups[g]
+            if j0 == first:
+                grouped[g] = grp_pool.tile([P, n * HID], BF16, name="grouped", align_bytes=64)
+            words = x_sb[c][:].rearrange("p i k -> p (i k)").bitcast(F32)
             dst = grouped[g][:].bitcast(F32).rearrange("p (i r u) -> p i r u", r=P, u=2)
-            for i0 in range(0, n, PAIR):
-                xt = xt_psum.tile([P, PAIR, 2, P], F32, name="xt")
-                for i in range(PAIR):
-                    w0 = (i0 + i) * (HID // 2)
-                    for u in range(2):
-                        nc.tensor.transpose(xt[:, i, u, :], words[:, w0 + u : w0 + HID // 2 : 2], ident[:])
-                nc.scalar.copy(out=dst[:, i0 : i0 + PAIR, :, :], in_=xt[:].rearrange("p i u r -> p i r u"))
+            xt = xt_psum.tile([P, PAIR, 2, P], F32, name="xt")
+            for i in range(PAIR):
+                w0 = (j0 + i - load_first[c]) * (HID // 2)
+                for u in range(2):
+                    nc.tensor.transpose(xt[:, i, u, :], words[:, w0 + u : w0 + HID // 2 : 2], ident[:])
+            nc.scalar.copy(out=dst[:, j0 - first : j0 - first + PAIR, :, :], in_=xt[:].rearrange("p i u r -> p i r u"))
+            if j0 + PAIR == first + n:
+                gather_factors(g)
+            if j0 + PAIR == load_first[c] + LOADS[c] and c + X_BUFS < len(LOADS):
+                load(c + X_BUFS)
 
         def quantize(g):
             n = groups[g][1]
@@ -104,52 +116,57 @@ def tile_flashphiattention_pa_t_kernel(tc, hidden_states, cos, sin, w_qk_words, 
                 qk[g].append((i0, m, bank))
 
         def add_bias(g):
-            s, within = groups[g][2:]
-            if within == 0:
-                out_sb[s] = out_pool.tile([P, 2, sum(STORES[s]), NOUT // 2], F32, name="out_sb")
+            n = groups[g][1]
+            out_sb[g] = out_pool.tile([P, 2, n, NOUT // 2], F32, name="out_sb")
             for i0, m, bank in qk[g]:
                 nc.vector.tensor_tensor(
-                    out=out_sb[s][:, :, within + i0 : within + i0 + m, :],
+                    out=out_sb[g][:, :, i0 : i0 + m, :],
                     in0=bank[:].rearrange("p i (a c) -> p a i c", a=2),
                     in1=bias[:].rearrange("p (a c) -> p a c", a=2).unsqueeze(2).broadcast_to([P, 2, m, NOUT // 2]),
                     op=ALU.add,
                 )
 
         def heads(g):
-            n, s, within = groups[g][1:]
-            return out_sb[s][:, :, within : within + n, :].rearrange("p a i (h d) -> p a i h d", d=HEAD)
+            return out_sb[g][:].rearrange("p a i (h d) -> p a (i h) d", d=HEAD)
+
+        def gather_factors(g):
+            j0, n = groups[g]
+            factors[g] = fac_pool.tile([P, 2, n, HALF], BF16, name="factors")
+            table, j = (cos_sin_early, j0) if j0 < EARLY else (cos_sin_late, j0 - EARLY)
+            nc.scalar.copy(out=factors[g][:], in_=table[:, :, j : j + n, :])
 
         def multiply(g):
-            j0, n = groups[g][:2]
-            prod[g] = mx_pool.tile([P, 2, 2, n, 2, 2, HALF], F32, name="prod")
-            for t, table in enumerate((cos_sb, sin_sb)):
-                factor = table[:, j0 : j0 + n, :].unsqueeze(2).broadcast_to([P, n, 4, HALF])
-                for a in range(2):
-                    nc.vector.tensor_tensor(
-                        out=prod[g][:, t, a, :, :, :, :].rearrange("p i h f j -> p i (h f) j"),
-                        in0=heads(g)[:, a, :, :, 0 : 2 * HALF],
-                        in1=factor,
-                        op=ALU.mult,
-                    )
+            n = groups[g][1]
+            prod[g] = mx_pool.tile([P, 2, 2, 2 * n, 2, HALF], F32, name="prod")
+            factor = factors[g][:].rearrange("p t i j -> p (t i) j").unsqueeze(2).broadcast_to([P, 2 * n, 4, HALF])
+            for a in range(2):
+                nc.vector.tensor_tensor(
+                    out=prod[g][:, :, a, :, :, :].rearrange("p t r f j -> p t (r f j)"),
+                    in0=heads(g)[:, a, :, 0 : 2 * HALF].unsqueeze(1).broadcast_to([P, 2, 2 * n, 2 * HALF]),
+                    in1=factor,
+                    op=ALU.mult,
+                )
 
-        def combine(g):
-            n, s, within = groups[g][1:]
-            nc.vector.tensor_tensor(
-                out=heads(g)[:, :, :, :, 0:HALF],
-                in0=prod[g][:, 0, :, :, :, 0, :],
-                in1=prod[g][:, 1, :, :, :, 1, :],
+        def combine_first(g, engine):
+            engine.tensor_tensor(
+                out=heads(g)[:, :, :, 0:HALF],
+                in0=prod[g][:, 0, :, :, 0, :],
+                in1=prod[g][:, 1, :, :, 1, :],
                 op=ALU.subtract,
             )
+
+        def combine_second(g):
             nc.vector.tensor_tensor(
-                out=heads(g)[:, :, :, :, HALF : 2 * HALF],
-                in0=prod[g][:, 0, :, :, :, 1, :],
-                in1=prod[g][:, 1, :, :, :, 0, :],
+                out=heads(g)[:, :, :, HALF : 2 * HALF],
+                in0=prod[g][:, 0, :, :, 1, :],
+                in1=prod[g][:, 1, :, :, 0, :],
                 op=ALU.add,
             )
-            if within + n == sum(STORES[s]):
-                j1 = groups[g][0] + n
-                for a in range(2):
-                    nc.sync.dma_start(out=out_hbm[a][:, j1 - within - n : j1, :], in_=out_sb[s][:, a, :, :])
+
+        def store(g):
+            j0, n = groups[g]
+            for a in range(2):
+                nc.sync.dma_start(out=out_hbm[a][:, j0 : j0 + n, :], in_=out_sb[g][:, a, :, :])
 
         make_identity(nc, ident[:])
         nc.vector.memset(bias_row[:], 0.0)
@@ -162,31 +179,46 @@ def tile_flashphiattention_pa_t_kernel(tc, hidden_states, cos, sin, w_qk_words, 
         )
         nc.sync.dma_start(out=bias_row[0:1, :], in_=b_qk.rearrange("(o n) -> o n", o=1))
         load(1)
-        load(2)
-        nc.sync.dma_start(out=cos_sb[:], in_=cos.rearrange("(p j) c -> p j c", p=P))
-        nc.sync.dma_start(out=sin_sb[:], in_=sin.rearrange("(p j) c -> p j c", p=P))
-        for g in range(3, X_BUFS):
-            load(g)
+        tables = [t.rearrange("(p j) c -> p j c", p=P) for t in (cos, sin)]
+        for t in range(2):
+            nc.sync.dma_start(out=cos_sin_early[:, t, :, :], in_=tables[t][:, :EARLY, :])
+        for c in range(2, X_BUFS):
+            if load_first[c] == EARLY:
+                for t in range(2):
+                    nc.sync.dma_start(out=cos_sin_late[:, t, :, :], in_=tables[t][:, EARLY:, :])
+            load(c)
         for q in range(1, 4):
             nc.vector.tensor_copy(
                 out=w_scales[32 * q : 32 * q + 4, 0, :].bitcast(I32), in_=w_scales[0:4, q, :].bitcast(I32)
             )
 
-        for i in range(-3, n_groups + 1):
+        transposed = 0
+        quantized = 0
+        for i in range(-1, n_groups + 1):
+            if i - 1 in SHARED:
+                combine_first(i - 1, nc.gpsimd)
             if 0 <= i < n_groups:
                 add_bias(i)
+                limit = groups[i][0] + groups[i][1] + max(Q_LEAD, groups[i][1])
+            elif i < 0:
+                limit = Q_LEAD
+            while quantized < n_groups and groups[quantized][0] < limit:
+                first, n = groups[quantized]
+                while transposed < min(TILES, first + n + min(T_LEAD, 6 + first)):
+                    transpose(transposed)
+                    transposed += PAIR
+                if quantized == 0:
+                    spread = qk_psum.tile([P, NOUT], F32, name="bank")
+                    nc.tensor.matmul(spread[:], lhsT=ones[:], rhs=bias_row[:], start=True, stop=True)
+                quantize(quantized)
+                if quantized == 0:
+                    nc.vector.tensor_copy(out=bias[:], in_=spread[:])
+                project(quantized)
+                quantized += 1
             if 0 <= i - 1 < n_groups:
-                combine(i - 1)
-            if i + 3 < n_groups:
-                transpose(i + 3)
-                if i + 3 + X_BUFS < n_groups:
-                    load(i + 3 + X_BUFS)
-            if i == -2:
-                spread = qk_psum.tile([P, NOUT], F32, name="bank")
-                nc.tensor.matmul(spread[:], lhsT=ones[:], rhs=bias_row[:], start=True, stop=True)
-                nc.vector.tensor_copy(out=bias[:], in_=spread[:])
-            if 0 <= i + 2 < n_groups:
-                quantize(i + 2)
-                project(i + 2)
+                if i - 1 not in SHARED:
+                    combine_first(i - 1, nc.vector)
+                combine_second(i - 1)
+                store(i - 1)
             if 0 <= i < n_groups:
                 multiply(i)

@@ -15,6 +15,7 @@ U8 = mybir.dt.uint8
 E5M2X4 = mybir.dt.float8_e5m2_x4
 E2M1X4 = mybir.dt.float4_e2m1fn_x4
 ALU = mybir.AluOpType
+ACT = mybir.ActivationFunctionType
 
 P = 128
 TILES = T // P
@@ -23,9 +24,10 @@ QUAD = 4
 GROUPS = [2, 2, 4] + [8] * 14 + [4, 4]
 LOADS = [2, 2] + [4] * 31
 EARLY = 16
-SHARED = range(3, 17)
+SHARED = range(3, 16)
 T_LEAD = 8
 Q_LEAD = 4
+POOL_ROWS = 24
 X_BUFS = 16
 
 
@@ -90,11 +92,16 @@ def tile_flashphiattention_pa_t_kernel(tc, hidden_states, cos, sin, w_qk_words, 
             if j0 + PAIR == load_first[c] + LOADS[c] and c + X_BUFS < len(LOADS):
                 load(c + X_BUFS)
 
-        def quantize(g):
+        def quantize(g, i0, i1):
             n = groups[g][1]
-            codes[g] = mx_pool.tile([P, n * P], U32, name="codes", align_bytes=64)
-            scales[g] = mx_pool.tile([P, n * P], U8, name="scales", align_bytes=64)
-            nc.vector.quantize_mx(out=codes[g][:].bitcast(E5M2X4), scales=scales[g][:], in_=grouped[g][:])
+            if i0 == 0:
+                codes[g] = mx_pool.tile([P, n * P], U32, name="codes", align_bytes=64)
+                scales[g] = mx_pool.tile([P, n * P], U8, name="scales", align_bytes=64)
+            nc.vector.quantize_mx(
+                out=codes[g][:, i0 * P : i1 * P].bitcast(E5M2X4),
+                scales=scales[g][:, i0 * P : i1 * P],
+                in_=grouped[g][:, i0 * HID : i1 * HID],
+            )
 
         def project(g):
             n = groups[g][1]
@@ -126,41 +133,37 @@ def tile_flashphiattention_pa_t_kernel(tc, hidden_states, cos, sin, w_qk_words, 
                     op=ALU.add,
                 )
 
-        def heads(g):
-            return out_sb[g][:].rearrange("p a i (h d) -> p a (i h) d", d=HEAD)
+        def rows(g):
+            return out_sb[g][:].rearrange("p a i (h d) -> p (a i h) d", d=HEAD)
 
         def gather_factors(g):
             j0, n = groups[g]
-            factors[g] = fac_pool.tile([P, 2, n, HALF], BF16, name="factors")
             table, j = (cos_sin_early, j0) if j0 < EARLY else (cos_sin_late, j0 - EARLY)
-            nc.scalar.copy(out=factors[g][:], in_=table[:, :, j : j + n, :])
+            factors[g] = fac_pool.tile([P, 2, n, 2, 2, HALF], BF16, name="factors")
+            nc.scalar.copy(
+                out=factors[g][:, 0, :, :, :, :].rearrange("p i h f j -> p i (h f) j"),
+                in_=table[:, 0, j : j + n, :].unsqueeze(2).broadcast_to([P, n, 4, HALF]),
+            )
+            sines = table[:, 1, j : j + n, :].unsqueeze(2).broadcast_to([P, n, 2, HALF])
+            nc.scalar.activation(out=factors[g][:, 1, :, :, 0, :], in_=sines, func=ACT.Copy, scale=-1.0)
+            nc.scalar.copy(out=factors[g][:, 1, :, :, 1, :], in_=sines)
 
         def multiply(g):
             n = groups[g][1]
-            prod[g] = mx_pool.tile([P, 2, 2, 2 * n, 2, HALF], F32, name="prod")
-            factor = factors[g][:].rearrange("p t i j -> p (t i) j").unsqueeze(2).broadcast_to([P, 2 * n, 4, HALF])
-            for a in range(2):
+            prod[g] = mx_pool.tile([P, 2, 4 * n, 2 * HALF], F32, name="prod")
+            halves = rows(g)[:, :, : 2 * HALF].rearrange("p r (f j) -> p r f j", f=2)
+            for t, source in enumerate((halves, halves[:, :, ::-1, :])):
+                factor = factors[g][:, t, :, :, :, :].rearrange("p i h f j -> p (i h f j)")
                 nc.vector.tensor_tensor(
-                    out=prod[g][:, :, a, :, :, :].rearrange("p t r f j -> p t (r f j)"),
-                    in0=heads(g)[:, a, :, 0 : 2 * HALF].unsqueeze(1).broadcast_to([P, 2, 2 * n, 2 * HALF]),
-                    in1=factor,
+                    out=prod[g][:, t, :, :],
+                    in0=source,
+                    in1=factor.unsqueeze(1).broadcast_to([P, 2, n * 4 * HALF]),
                     op=ALU.mult,
                 )
 
-        def combine_first(g, engine):
+        def combine(g, engine, r0, r1):
             engine.tensor_tensor(
-                out=heads(g)[:, :, :, 0:HALF],
-                in0=prod[g][:, 0, :, :, 0, :],
-                in1=prod[g][:, 1, :, :, 1, :],
-                op=ALU.subtract,
-            )
-
-        def combine_second(g):
-            nc.vector.tensor_tensor(
-                out=heads(g)[:, :, :, HALF : 2 * HALF],
-                in0=prod[g][:, 0, :, :, 1, :],
-                in1=prod[g][:, 1, :, :, 0, :],
-                op=ALU.add,
+                out=rows(g)[:, r0:r1, : 2 * HALF], in0=prod[g][:, 0, r0:r1, :], in1=prod[g][:, 1, r0:r1, :], op=ALU.add
             )
 
         def store(g):
@@ -193,32 +196,35 @@ def tile_flashphiattention_pa_t_kernel(tc, hidden_states, cos, sin, w_qk_words, 
             )
 
         transposed = 0
-        quantized = 0
+        projected = 0
+        ahead = 0
         for i in range(-1, n_groups + 1):
             if i - 1 in SHARED:
-                combine_first(i - 1, nc.gpsimd)
+                combine(i - 1, nc.gpsimd, 0, POOL_ROWS)
             if 0 <= i < n_groups:
                 add_bias(i)
                 limit = groups[i][0] + groups[i][1] + max(Q_LEAD, groups[i][1])
             elif i < 0:
                 limit = Q_LEAD
-            while quantized < n_groups and groups[quantized][0] < limit:
-                first, n = groups[quantized]
+            while projected < n_groups and groups[projected][0] < limit:
+                first, n = groups[projected]
                 while transposed < min(TILES, first + n + min(T_LEAD, 6 + first)):
                     transpose(transposed)
                     transposed += PAIR
-                if quantized == 0:
+                if projected == 0:
                     spread = qk_psum.tile([P, NOUT], F32, name="bank")
                     nc.tensor.matmul(spread[:], lhsT=ones[:], rhs=bias_row[:], start=True, stop=True)
-                quantize(quantized)
-                if quantized == 0:
+                quantize(projected, ahead, n)
+                ahead = 0
+                if projected == 0:
                     nc.vector.tensor_copy(out=bias[:], in_=spread[:])
-                project(quantized)
-                quantized += 1
+                project(projected)
+                projected += 1
             if 0 <= i - 1 < n_groups:
-                if i - 1 not in SHARED:
-                    combine_first(i - 1, nc.vector)
-                combine_second(i - 1)
+                combine(i - 1, nc.vector, POOL_ROWS if i - 1 in SHARED else 0, 4 * groups[i - 1][1])
                 store(i - 1)
             if 0 <= i < n_groups:
                 multiply(i)
+            if i in SHARED and projected < n_groups:
+                ahead = groups[projected][1] // 2
+                quantize(projected, 0, ahead)

@@ -19,36 +19,42 @@ ACT = mybir.ActivationFunctionType
 
 P = 128
 TILES = T // P
+WORDS = HID // 2
+HEADS = NOUT // HEAD
 PAIR = 2
 QUAD = 4
-GROUPS = [2, 2, 4] + [8] * 14 + [4, 4]
-LOADS = [2, 2] + [4] * 31
+FULL = 8
+
+GROUPS = [PAIR, PAIR, QUAD] + [FULL] * 14 + [QUAD, QUAD]
+HEAD_LOADS = [PAIR] * 6 + [QUAD] * 5
+LOADS = HEAD_LOADS + [FULL] * 12
+RING = 4
 EARLY = 16
-SHARED = range(3, 16)
 T_LEAD = 8
-Q_LEAD = 4
-POOL_ROWS = 24
-X_BUFS = 16
+FIRST_T_LEAD = 6
+MIN_MM_LEAD = 4
+SHARED = [g for g in range(len(GROUPS) - 1) if GROUPS[g] == FULL and GROUPS[g + 1] == FULL]
+POOL_ROWS = 28
 
 
 def tile_flashphiattention_pa_t_kernel(tc, hidden_states, cos, sin, w_qk_words, w_qk_scales, b_qk, out_0, out_1):
     nc = tc.nc
-    groups = []
-    first = 0
-    for n in GROUPS:
-        groups.append((first, n))
-        first += n
-    assert first == TILES
-    n_groups = len(groups)
+    n_groups = len(GROUPS)
+    group_first = [sum(GROUPS[:g]) for g in range(n_groups)]
+    load_first = [sum(LOADS[:c]) for c in range(len(LOADS))]
+    group_of = [g for g, n in enumerate(GROUPS) for i in range(n)]
+    load_of = [c for c, n in enumerate(LOADS) for i in range(n)]
+    assert sum(GROUPS) == TILES and sum(LOADS) == TILES
 
     x_hbm = hidden_states.rearrange("(p j) k -> p j k", p=P)
-    out_hbm = [o.rearrange("(p j) h d -> p j (h d)", p=P) for o in (out_0, out_1)]
+    tables_hbm = [table.rearrange("(p j) c -> p j c", p=P) for table in (cos, sin)]
+    out_hbm = [out.rearrange("(p j) h d -> p j (h d)", p=P) for out in (out_0, out_1)]
 
     with ExitStack() as ctx:
         const = ctx.enter_context(tc.tile_pool(name="const", bufs=1))
-        x_pool = ctx.enter_context(tc.tile_pool(name="x", bufs=X_BUFS))
+        x_pool = ctx.enter_context(tc.tile_pool(name="x", bufs=RING))
         mx_pool = ctx.enter_context(tc.tile_pool(name="mx", bufs=3))
-        out_pool = ctx.enter_context(tc.tile_pool(name="out", bufs=14))
+        out_pool = ctx.enter_context(tc.tile_pool(name="out", bufs=n_groups))
         grp_pool = ctx.enter_context(tc.tile_pool(name="grp", bufs=4))
         fac_pool = ctx.enter_context(tc.tile_pool(name="fac", bufs=6))
         xt_psum = ctx.enter_context(tc.psum_pool(name="xt", bufs=4))
@@ -66,37 +72,49 @@ def tile_flashphiattention_pa_t_kernel(tc, hidden_states, cos, sin, w_qk_words, 
 
         x_sb, grouped, codes, scales, qk, out_sb, prod, factors = {}, {}, {}, {}, {}, {}, {}, {}
 
-        load_first = [sum(LOADS[:c]) for c in range(len(LOADS))]
-        group_of = [g for g, n in enumerate(GROUPS) for i in range(n)]
-        load_of = [c for c, n in enumerate(LOADS) for i in range(n)]
-
         def load(c):
-            x_sb[c] = x_pool.tile([P, LOADS[c], HID], BF16, name="x_sb")
+            pool, name = (const, "x_head%d" % c) if c < len(HEAD_LOADS) else (x_pool, "x_ring")
+            x_sb[c] = pool.tile([P, LOADS[c], HID], BF16, name=name)
             nc.sync.dma_start(out=x_sb[c][:], in_=x_hbm[:, load_first[c] : load_first[c] + LOADS[c], :])
 
-        def transpose(j0):
+        def load_tables(dst, j0, j1):
+            for t in range(2):
+                nc.sync.dma_start(out=dst[:, t, :, :], in_=tables_hbm[t][:, j0:j1, :])
+
+        def lay_out_factors(g):
+            j0, n = group_first[g], GROUPS[g]
+            table, j = (cos_sin_early, j0) if j0 < EARLY else (cos_sin_late, j0 - EARLY)
+            factors[g] = fac_pool.tile([P, 2, n, 2, 2, HALF], BF16, name="factors")
+            nc.scalar.copy(
+                out=factors[g][:, 0, :, :, :, :].rearrange("p i h f j -> p i (h f) j"),
+                in_=table[:, 0, j : j + n, :].unsqueeze(2).broadcast_to([P, n, 4, HALF]),
+            )
+            sines = table[:, 1, j : j + n, :].unsqueeze(2).broadcast_to([P, n, 2, HALF])
+            nc.scalar.activation(out=factors[g][:, 1, :, :, 0, :], in_=sines, func=ACT.Copy, scale=-1.0)
+            nc.scalar.copy(out=factors[g][:, 1, :, :, 1, :], in_=sines)
+
+        def transpose_pair(j0):
             g, c = group_of[j0], load_of[j0]
-            first, n = groups[g]
-            if j0 == first:
+            i0, n = j0 - group_first[g], GROUPS[g]
+            if i0 == 0:
                 grouped[g] = grp_pool.tile([P, n * HID], BF16, name="grouped", align_bytes=64)
             words = x_sb[c][:].rearrange("p i k -> p (i k)").bitcast(F32)
             dst = grouped[g][:].bitcast(F32).rearrange("p (i r u) -> p i r u", r=P, u=2)
             xt = xt_psum.tile([P, PAIR, 2, P], F32, name="xt")
             for i in range(PAIR):
-                w0 = (j0 + i - load_first[c]) * (HID // 2)
+                w0 = (j0 + i - load_first[c]) * WORDS
                 for u in range(2):
-                    nc.tensor.transpose(xt[:, i, u, :], words[:, w0 + u : w0 + HID // 2 : 2], ident[:])
-            nc.scalar.copy(out=dst[:, j0 - first : j0 - first + PAIR, :, :], in_=xt[:].rearrange("p i u r -> p i r u"))
-            if j0 + PAIR == first + n:
-                gather_factors(g)
-            if j0 + PAIR == load_first[c] + LOADS[c] and c + X_BUFS < len(LOADS):
-                load(c + X_BUFS)
+                    nc.tensor.transpose(xt[:, i, u, :], words[:, w0 + u : w0 + WORDS : 2], ident[:])
+            nc.scalar.copy(out=dst[:, i0 : i0 + PAIR, :, :], in_=xt[:].rearrange("p i u r -> p i r u"))
+            if i0 + PAIR == n:
+                lay_out_factors(g)
+            if j0 + PAIR == load_first[c] + LOADS[c] and len(HEAD_LOADS) <= c < len(LOADS) - RING:
+                load(c + RING)
 
         def quantize(g, i0, i1):
-            n = groups[g][1]
             if i0 == 0:
-                codes[g] = mx_pool.tile([P, n * P], U32, name="codes", align_bytes=64)
-                scales[g] = mx_pool.tile([P, n * P], U8, name="scales", align_bytes=64)
+                codes[g] = mx_pool.tile([P, GROUPS[g] * P], U32, name="codes", align_bytes=64)
+                scales[g] = mx_pool.tile([P, GROUPS[g] * P], U8, name="scales", align_bytes=64)
             nc.vector.quantize_mx(
                 out=codes[g][:, i0 * P : i1 * P].bitcast(E5M2X4),
                 scales=scales[g][:, i0 * P : i1 * P],
@@ -104,10 +122,9 @@ def tile_flashphiattention_pa_t_kernel(tc, hidden_states, cos, sin, w_qk_words, 
             )
 
         def project(g):
-            n = groups[g][1]
             qk[g] = []
-            for i0 in range(0, n, QUAD):
-                m = min(QUAD, n - i0)
+            for i0 in range(0, GROUPS[g], QUAD):
+                m = min(QUAD, GROUPS[g] - i0)
                 bank = qk_psum.tile([P, m, NOUT], F32, name="bank")
                 for i in range(m):
                     cols = slice((i0 + i) * P, (i0 + i + 1) * P)
@@ -123,8 +140,7 @@ def tile_flashphiattention_pa_t_kernel(tc, hidden_states, cos, sin, w_qk_words, 
                 qk[g].append((i0, m, bank))
 
         def add_bias(g):
-            n = groups[g][1]
-            out_sb[g] = out_pool.tile([P, 2, n, NOUT // 2], F32, name="out_sb")
+            out_sb[g] = out_pool.tile([P, 2, GROUPS[g], NOUT // 2], F32, name="out_sb")
             for i0, m, bank in qk[g]:
                 nc.vector.tensor_tensor(
                     out=out_sb[g][:, :, i0 : i0 + m, :],
@@ -133,26 +149,14 @@ def tile_flashphiattention_pa_t_kernel(tc, hidden_states, cos, sin, w_qk_words, 
                     op=ALU.add,
                 )
 
-        def rows(g):
+        def head_rows(g):
             return out_sb[g][:].rearrange("p a i (h d) -> p (a i h) d", d=HEAD)
 
-        def gather_factors(g):
-            j0, n = groups[g]
-            table, j = (cos_sin_early, j0) if j0 < EARLY else (cos_sin_late, j0 - EARLY)
-            factors[g] = fac_pool.tile([P, 2, n, 2, 2, HALF], BF16, name="factors")
-            nc.scalar.copy(
-                out=factors[g][:, 0, :, :, :, :].rearrange("p i h f j -> p i (h f) j"),
-                in_=table[:, 0, j : j + n, :].unsqueeze(2).broadcast_to([P, n, 4, HALF]),
-            )
-            sines = table[:, 1, j : j + n, :].unsqueeze(2).broadcast_to([P, n, 2, HALF])
-            nc.scalar.activation(out=factors[g][:, 1, :, :, 0, :], in_=sines, func=ACT.Copy, scale=-1.0)
-            nc.scalar.copy(out=factors[g][:, 1, :, :, 1, :], in_=sines)
-
         def multiply(g):
-            n = groups[g][1]
-            prod[g] = mx_pool.tile([P, 2, 4 * n, 2 * HALF], F32, name="prod")
-            halves = rows(g)[:, :, : 2 * HALF].rearrange("p r (f j) -> p r f j", f=2)
-            for t, source in enumerate((halves, halves[:, :, ::-1, :])):
+            n = GROUPS[g]
+            prod[g] = mx_pool.tile([P, 2, HEADS * n, 2 * HALF], F32, name="prod")
+            pieces = head_rows(g)[:, :, : 2 * HALF].rearrange("p r (f j) -> p r f j", f=2)
+            for t, source in enumerate((pieces, pieces[:, :, ::-1, :])):
                 factor = factors[g][:, t, :, :, :, :].rearrange("p i h f j -> p (i h f j)")
                 nc.vector.tensor_tensor(
                     out=prod[g][:, t, :, :],
@@ -163,11 +167,11 @@ def tile_flashphiattention_pa_t_kernel(tc, hidden_states, cos, sin, w_qk_words, 
 
         def combine(g, engine, r0, r1):
             engine.tensor_tensor(
-                out=rows(g)[:, r0:r1, : 2 * HALF], in0=prod[g][:, 0, r0:r1, :], in1=prod[g][:, 1, r0:r1, :], op=ALU.add
+                out=head_rows(g)[:, r0:r1, : 2 * HALF], in0=prod[g][:, 0, r0:r1, :], in1=prod[g][:, 1, r0:r1, :], op=ALU.add
             )
 
         def store(g):
-            j0, n = groups[g]
+            j0, n = group_first[g], GROUPS[g]
             for a in range(2):
                 nc.sync.dma_start(out=out_hbm[a][:, j0 : j0 + n, :], in_=out_sb[g][:, a, :, :])
 
@@ -175,24 +179,22 @@ def tile_flashphiattention_pa_t_kernel(tc, hidden_states, cos, sin, w_qk_words, 
         nc.vector.memset(bias_row[:], 0.0)
         nc.vector.memset(ones[:], 1.0)
         load(0)
+        load(1)
         nc.sync.dma_start(out=w_words[:].bitcast(I32), in_=w_qk_words[0].bitcast(I32))
         nc.sync.dma_start(
             out=w_scales[0:4, :, :].bitcast(I32),
             in_=w_qk_scales[0].rearrange("(q r) n -> r q n", r=4).bitcast(I32),
         )
         nc.sync.dma_start(out=bias_row[0:1, :], in_=b_qk.rearrange("(o n) -> o n", o=1))
-        load(1)
-        tables = [t.rearrange("(p j) c -> p j c", p=P) for t in (cos, sin)]
-        for t in range(2):
-            nc.sync.dma_start(out=cos_sin_early[:, t, :, :], in_=tables[t][:, :EARLY, :])
-        for c in range(2, X_BUFS):
+        load_tables(cos_sin_early, 0, EARLY)
+        for c in range(2, len(HEAD_LOADS) + RING):
             if load_first[c] == EARLY:
-                for t in range(2):
-                    nc.sync.dma_start(out=cos_sin_late[:, t, :, :], in_=tables[t][:, EARLY:, :])
+                load_tables(cos_sin_late, EARLY, TILES)
             load(c)
-        for q in range(1, 4):
+        for quadrant in range(1, 4):
             nc.vector.tensor_copy(
-                out=w_scales[32 * q : 32 * q + 4, 0, :].bitcast(I32), in_=w_scales[0:4, q, :].bitcast(I32)
+                out=w_scales[32 * quadrant : 32 * quadrant + 4, 0, :].bitcast(I32),
+                in_=w_scales[0:4, quadrant, :].bitcast(I32),
             )
 
         transposed = 0
@@ -201,30 +203,30 @@ def tile_flashphiattention_pa_t_kernel(tc, hidden_states, cos, sin, w_qk_words, 
         for i in range(-1, n_groups + 1):
             if i - 1 in SHARED:
                 combine(i - 1, nc.gpsimd, 0, POOL_ROWS)
+            if i == 0:
+                nc.vector.tensor_copy(out=bias[:], in_=spread[:])
             if 0 <= i < n_groups:
                 add_bias(i)
-                limit = groups[i][0] + groups[i][1] + max(Q_LEAD, groups[i][1])
+                limit = group_first[i] + GROUPS[i] + max(MIN_MM_LEAD, GROUPS[i])
             elif i < 0:
-                limit = Q_LEAD
-            while projected < n_groups and groups[projected][0] < limit:
-                first, n = groups[projected]
-                while transposed < min(TILES, first + n + min(T_LEAD, 6 + first)):
-                    transpose(transposed)
+                limit = MIN_MM_LEAD
+            while projected < n_groups and group_first[projected] < limit:
+                end = group_first[projected] + GROUPS[projected]
+                while transposed < min(TILES, end + (T_LEAD if projected else FIRST_T_LEAD)):
+                    transpose_pair(transposed)
                     transposed += PAIR
                 if projected == 0:
                     spread = qk_psum.tile([P, NOUT], F32, name="bank")
                     nc.tensor.matmul(spread[:], lhsT=ones[:], rhs=bias_row[:], start=True, stop=True)
-                quantize(projected, ahead, n)
+                quantize(projected, ahead, GROUPS[projected])
                 ahead = 0
-                if projected == 0:
-                    nc.vector.tensor_copy(out=bias[:], in_=spread[:])
                 project(projected)
                 projected += 1
-            if 0 <= i - 1 < n_groups:
-                combine(i - 1, nc.vector, POOL_ROWS if i - 1 in SHARED else 0, 4 * groups[i - 1][1])
+            if i >= 1:
+                combine(i - 1, nc.vector, POOL_ROWS if i - 1 in SHARED else 0, HEADS * GROUPS[i - 1])
                 store(i - 1)
             if 0 <= i < n_groups:
                 multiply(i)
-            if i in SHARED and projected < n_groups:
-                ahead = groups[projected][1] // 2
+            if i >= 0 and projected < n_groups:
+                ahead = GROUPS[projected] // 2
                 quantize(projected, 0, ahead)

from contextlib import ExitStack

import concourse.mybir as mybir
from concourse.masks import make_identity

T, HID, NOUT = 16384, 512, 128
HEAD, HALF = 32, 8
FLOPS = 2 * T * HID * NOUT

F32 = mybir.dt.float32
BF16 = mybir.dt.bfloat16
I32 = mybir.dt.int32
U32 = mybir.dt.uint32
U8 = mybir.dt.uint8
E5M2X4 = mybir.dt.float8_e5m2_x4
E2M1X4 = mybir.dt.float4_e2m1fn_x4
ALU = mybir.AluOpType
ACT = mybir.ActivationFunctionType

P = 128
TILES = T // P
WORDS = HID // 2
HEADS = NOUT // HEAD
PAIR = 2
QUAD = 4
FULL = 8

GROUPS = [PAIR, PAIR, QUAD] + [FULL] * 14 + [QUAD, QUAD]
HEAD_LOADS = [PAIR] * 6 + [QUAD] * 5
LOADS = HEAD_LOADS + [FULL] * 12
RING = 4
EARLY = 16
T_LEAD = 8
FIRST_T_LEAD = 6
MIN_MM_LEAD = 4
SHARED = [g for g in range(len(GROUPS) - 1) if GROUPS[g] == FULL and GROUPS[g + 1] == FULL]
POOL_ROWS = 28


def tile_flashphiattention_pa_t_kernel(tc, hidden_states, cos, sin, w_qk_words, w_qk_scales, b_qk, out_0, out_1):
    nc = tc.nc
    n_groups = len(GROUPS)
    group_first = [sum(GROUPS[:g]) for g in range(n_groups)]
    load_first = [sum(LOADS[:c]) for c in range(len(LOADS))]
    group_of = [g for g, n in enumerate(GROUPS) for i in range(n)]
    load_of = [c for c, n in enumerate(LOADS) for i in range(n)]
    assert sum(GROUPS) == TILES and sum(LOADS) == TILES

    x_hbm = hidden_states.rearrange("(p j) k -> p j k", p=P)
    tables_hbm = [table.rearrange("(p j) c -> p j c", p=P) for table in (cos, sin)]
    out_hbm = [out.rearrange("(p j) h d -> p j (h d)", p=P) for out in (out_0, out_1)]

    with ExitStack() as ctx:
        const = ctx.enter_context(tc.tile_pool(name="const", bufs=1))
        x_pool = ctx.enter_context(tc.tile_pool(name="x", bufs=RING))
        mx_pool = ctx.enter_context(tc.tile_pool(name="mx", bufs=3))
        out_pool = ctx.enter_context(tc.tile_pool(name="out", bufs=n_groups))
        grp_pool = ctx.enter_context(tc.tile_pool(name="grp", bufs=4))
        fac_pool = ctx.enter_context(tc.tile_pool(name="fac", bufs=6))
        xt_psum = ctx.enter_context(tc.psum_pool(name="xt", bufs=4))
        qk_psum = ctx.enter_context(tc.psum_pool(name="qk", bufs=4))
        ctx.enter_context(tc.manual_schedule())

        ident = const.tile([P, P], F32, name="ident")
        w_words = const.tile([P, 2 * NOUT], U8, name="w_words", align_bytes=64)
        w_scales = const.tile([P, 4, NOUT], U8, name="w_scales", align_bytes=64)
        bias_row = const.tile([P, NOUT], BF16, name="bias_row")
        ones = const.tile([P, P], BF16, name="ones")
        bias = const.tile([P, NOUT], F32, name="bias")
        cos_sin_early = const.tile([P, 2, EARLY, HALF], BF16, name="cos_sin_early")
        cos_sin_late = const.tile([P, 2, TILES - EARLY, HALF], BF16, name="cos_sin_late")

        x_sb, grouped, codes, scales, qk, out_sb, prod, factors = {}, {}, {}, {}, {}, {}, {}, {}

        def load(c):
            pool, name = (const, "x_head%d" % c) if c < len(HEAD_LOADS) else (x_pool, "x_ring")
            x_sb[c] = pool.tile([P, LOADS[c], HID], BF16, name=name)
            nc.sync.dma_start(out=x_sb[c][:], in_=x_hbm[:, load_first[c] : load_first[c] + LOADS[c], :])

        def load_tables(dst, j0, j1):
            for t in range(2):
                nc.sync.dma_start(out=dst[:, t, :, :], in_=tables_hbm[t][:, j0:j1, :])

        def lay_out_factors(g):
            j0, n = group_first[g], GROUPS[g]
            table, j = (cos_sin_early, j0) if j0 < EARLY else (cos_sin_late, j0 - EARLY)
            factors[g] = fac_pool.tile([P, 2, n, 2, 2, HALF], BF16, name="factors")
            nc.scalar.copy(
                out=factors[g][:, 0, :, :, :, :].rearrange("p i h f j -> p i (h f) j"),
                in_=table[:, 0, j : j + n, :].unsqueeze(2).broadcast_to([P, n, 4, HALF]),
            )
            sines = table[:, 1, j : j + n, :].unsqueeze(2).broadcast_to([P, n, 2, HALF])
            nc.scalar.activation(out=factors[g][:, 1, :, :, 0, :], in_=sines, func=ACT.Copy, scale=-1.0)
            nc.scalar.copy(out=factors[g][:, 1, :, :, 1, :], in_=sines)

        def transpose_pair(j0):
            g, c = group_of[j0], load_of[j0]
            i0, n = j0 - group_first[g], GROUPS[g]
            if i0 == 0:
                grouped[g] = grp_pool.tile([P, n * HID], BF16, name="grouped", align_bytes=64)
            words = x_sb[c][:].rearrange("p i k -> p (i k)").bitcast(F32)
            dst = grouped[g][:].bitcast(F32).rearrange("p (i r u) -> p i r u", r=P, u=2)
            xt = xt_psum.tile([P, PAIR, 2, P], F32, name="xt")
            for i in range(PAIR):
                w0 = (j0 + i - load_first[c]) * WORDS
                for u in range(2):
                    nc.tensor.transpose(xt[:, i, u, :], words[:, w0 + u : w0 + WORDS : 2], ident[:])
            nc.scalar.copy(out=dst[:, i0 : i0 + PAIR, :, :], in_=xt[:].rearrange("p i u r -> p i r u"))
            if i0 + PAIR == n:
                lay_out_factors(g)
            if j0 + PAIR == load_first[c] + LOADS[c] and len(HEAD_LOADS) <= c < len(LOADS) - RING:
                load(c + RING)

        def quantize(g, i0, i1):
            if i0 == 0:
                codes[g] = mx_pool.tile([P, GROUPS[g] * P], U32, name="codes", align_bytes=64)
                scales[g] = mx_pool.tile([P, GROUPS[g] * P], U8, name="scales", align_bytes=64)
            nc.vector.quantize_mx(
                out=codes[g][:, i0 * P : i1 * P].bitcast(E5M2X4),
                scales=scales[g][:, i0 * P : i1 * P],
                in_=grouped[g][:, i0 * HID : i1 * HID],
            )

        def project(g):
            qk[g] = []
            for i0 in range(0, GROUPS[g], QUAD):
                m = min(QUAD, GROUPS[g] - i0)
                bank = qk_psum.tile([P, m, NOUT], F32, name="bank")
                for i in range(m):
                    cols = slice((i0 + i) * P, (i0 + i + 1) * P)
                    nc.tensor.matmul_mx(
                        out=bank[:, i, :],
                        lhsT=codes[g][:, cols].bitcast(E5M2X4),
                        lhsT_scale=scales[g][:, cols],
                        rhs=w_words[:].bitcast(E2M1X4),
                        rhs_scale=w_scales[:, 0, :],
                        start=True,
                        stop=True,
                    )
                qk[g].append((i0, m, bank))

        def add_bias(g):
            out_sb[g] = out_pool.tile([P, 2, GROUPS[g], NOUT // 2], F32, name="out_sb")
            for i0, m, bank in qk[g]:
                nc.vector.tensor_tensor(
                    out=out_sb[g][:, :, i0 : i0 + m, :],
                    in0=bank[:].rearrange("p i (a c) -> p a i c", a=2),
                    in1=bias[:].rearrange("p (a c) -> p a c", a=2).unsqueeze(2).broadcast_to([P, 2, m, NOUT // 2]),
                    op=ALU.add,
                )

        def head_rows(g):
            return out_sb[g][:].rearrange("p a i (h d) -> p (a i h) d", d=HEAD)

        def multiply(g):
            n = GROUPS[g]
            prod[g] = mx_pool.tile([P, 2, HEADS * n, 2 * HALF], F32, name="prod")
            pieces = head_rows(g)[:, :, : 2 * HALF].rearrange("p r (f j) -> p r f j", f=2)
            for t, source in enumerate((pieces, pieces[:, :, ::-1, :])):
                factor = factors[g][:, t, :, :, :, :].rearrange("p i h f j -> p (i h f j)")
                nc.vector.tensor_tensor(
                    out=prod[g][:, t, :, :],
                    in0=source,
                    in1=factor.unsqueeze(1).broadcast_to([P, 2, n * 4 * HALF]),
                    op=ALU.mult,
                )

        def combine(g, engine, r0, r1):
            engine.tensor_tensor(
                out=head_rows(g)[:, r0:r1, : 2 * HALF], in0=prod[g][:, 0, r0:r1, :], in1=prod[g][:, 1, r0:r1, :], op=ALU.add
            )

        def store(g):
            j0, n = group_first[g], GROUPS[g]
            for a in range(2):
                nc.sync.dma_start(out=out_hbm[a][:, j0 : j0 + n, :], in_=out_sb[g][:, a, :, :])

        make_identity(nc, ident[:])
        nc.vector.memset(bias_row[:], 0.0)
        nc.vector.memset(ones[:], 1.0)
        load(0)
        load(1)
        nc.sync.dma_start(out=w_words[:].bitcast(I32), in_=w_qk_words[0].bitcast(I32))
        nc.sync.dma_start(
            out=w_scales[0:4, :, :].bitcast(I32),
            in_=w_qk_scales[0].rearrange("(q r) n -> r q n", r=4).bitcast(I32),
        )
        nc.sync.dma_start(out=bias_row[0:1, :], in_=b_qk.rearrange("(o n) -> o n", o=1))
        load_tables(cos_sin_early, 0, EARLY)
        for c in range(2, len(HEAD_LOADS) + RING):
            if load_first[c] == EARLY:
                load_tables(cos_sin_late, EARLY, TILES)
            load(c)
        for quadrant in range(1, 4):
            nc.vector.tensor_copy(
                out=w_scales[32 * quadrant : 32 * quadrant + 4, 0, :].bitcast(I32),
                in_=w_scales[0:4, quadrant, :].bitcast(I32),
            )

        transposed = 0
        projected = 0
        ahead = 0
        for i in range(-1, n_groups + 1):
            if i - 1 in SHARED:
                combine(i - 1, nc.gpsimd, 0, POOL_ROWS)
            if i == 0:
                nc.vector.tensor_copy(out=bias[:], in_=spread[:])
            if 0 <= i < n_groups:
                add_bias(i)
                limit = group_first[i] + GROUPS[i] + max(MIN_MM_LEAD, GROUPS[i])
            elif i < 0:
                limit = MIN_MM_LEAD
            while projected < n_groups and group_first[projected] < limit:
                end = group_first[projected] + GROUPS[projected]
                while transposed < min(TILES, end + (T_LEAD if projected else FIRST_T_LEAD)):
                    transpose_pair(transposed)
                    transposed += PAIR
                if projected == 0:
                    spread = qk_psum.tile([P, NOUT], F32, name="bank")
                    nc.tensor.matmul(spread[:], lhsT=ones[:], rhs=bias_row[:], start=True, stop=True)
                quantize(projected, ahead, GROUPS[projected])
                ahead = 0
                project(projected)
                projected += 1
            if i >= 1:
                combine(i - 1, nc.vector, POOL_ROWS if i - 1 in SHARED else 0, HEADS * GROUPS[i - 1])
                store(i - 1)
            if 0 <= i < n_groups:
                multiply(i)
            if i >= 0 and projected < n_groups:
                ahead = GROUPS[projected] // 2
                quantize(projected, 0, ahead)
